import numpy as np
import ml_dtypes


def mxq(x, axis, fmt="e4m3"):
    dtype, down = {"e4m3": (ml_dtypes.float8_e4m3fn, 7), "e5m2": (ml_dtypes.float8_e5m2, 14)}[fmt]
    v = np.moveaxis(np.asarray(x, np.float32).astype(ml_dtypes.bfloat16).astype(np.float64), axis, -1)
    blocks = v.reshape(v.shape[:-1] + (-1, 32))
    amax = np.abs(blocks).max(-1, keepdims=True)
    byte = np.maximum(np.where(amax > 0, np.frexp(amax)[1] - 1 + 127, 0) - down, 1)
    scale = np.exp2(byte - 127.0)
    codes = (blocks / scale).astype(np.float32).astype(dtype).astype(np.float64)
    return np.moveaxis((codes * scale).reshape(v.shape), -1, axis)


WIDE = False


def mx_kscale(k):
    if not WIDE:
        return np.ones(k)
    levels = np.array([10, -10, 5, -5, 0])
    a = np.random.permutation(np.resize(levels, k // 512 * 4)).reshape(k // 512, 4)
    idx = np.arange(k)
    return np.exp2(a[idx // 512, idx % 128 // 32])


BF16 = ml_dtypes.bfloat16


def bf(x):
    return np.asarray(x, np.float32).astype(BF16)


def f64(x):
    return np.asarray(x).astype(np.float64)


E2M1 = np.array([0.0, 0.5, 1.0, 1.5, 2.0, 3.0, 4.0, 6.0, -0.0, -0.5, -1.0, -1.5, -2.0, -3.0, -4.0, -6.0])


def pack_weight(w, fmt):
    k, n = w.shape
    w = f64(bf(w)).reshape(k // 32, 32, n)
    amax = np.abs(w).max(1)
    if fmt == "e4m3":
        byte = np.frexp(amax)[1] - 1 + 127 - 7
    else:
        mant, ex = np.frexp(amax / 6.0)
        byte = np.where(mant > 0.5, ex, ex - 1) + 127
    byte = np.clip(np.where(amax > 0, byte, 1), 1, 254)
    scaled = (w * np.exp2(127.0 - byte)[:, None, :]).reshape(k, n).astype(np.float32)
    by_word = np.ascontiguousarray(scaled.reshape(k // 512, 128, 4, n).transpose(0, 1, 3, 2))
    if fmt == "e4m3":
        words = by_word.astype(ml_dtypes.float8_e4m3fn).view(np.uint8)
    else:
        c = by_word.astype(ml_dtypes.float4_e2m1fn).view(np.uint8) & 0xF
        words = c[..., 0::2] | (c[..., 1::2] << 4)
    return np.ascontiguousarray(words), np.ascontiguousarray(byte.astype(np.uint8).reshape(k // 512, 16, n))


def unpack_weight(words, scales, fmt):
    g, p, n, _ = words.shape
    if fmt == "e4m3":
        vals = np.ascontiguousarray(words).view(ml_dtypes.float8_e4m3fn).astype(np.float64)
    else:
        nib = np.empty((g, p, n, 4), np.uint8)
        nib[..., 0::2] = words & 0xF
        nib[..., 1::2] = words >> 4
        vals = E2M1[nib]
    vals = vals * np.repeat(np.exp2(scales.astype(np.float64) - 127.0), 8, axis=1)[..., None]
    return vals.transpose(0, 1, 3, 2).reshape(g * 512, n)


N_FFT, B, T = 1024, 16, 128
STRIDE = N_FFT + 1
L = T * STRIDE
FMT = "e4m3"


def _fourier_kernels(n_fft):
    s = np.arange(n_fft, dtype=np.float64)
    k = np.arange(n_fft, dtype=np.float64)[:, None]
    ang = 2.0 * np.pi * k * s / n_fft
    return np.sin(ang), np.cos(ang)


def setup_inputs():
    s = mx_kscale(N_FFT)
    sx = np.concatenate([s, np.ones(1)])
    x = (np.random.standard_normal((1, B, T, STRIDE)) * sx).reshape(1, B, L)
    ws, wc = _fourier_kernels(N_FFT)
    wsin = (ws + 0.5 * np.random.standard_normal((N_FFT, N_FFT))) / np.sqrt(N_FFT) / s[None, :]
    wcos = (wc + 0.5 * np.random.standard_normal((N_FFT, N_FFT))) / np.sqrt(N_FFT) / s[None, :]
    wsin_words, wsin_scales = pack_weight(np.ascontiguousarray(wsin.T), FMT)
    wcos_words, wcos_scales = pack_weight(np.ascontiguousarray(wcos.T), FMT)
    return {"x": bf(x), "wsin_words": wsin_words, "wsin_scales": wsin_scales,
            "wcos_words": wcos_words, "wcos_scales": wcos_scales}


def reference(x, wsin_words, wsin_scales, wcos_words, wcos_scales):
    sig = f64(x)[0]
    frames = sig.reshape(B, T, STRIDE)[..., :N_FFT]
    fq = mxq(frames, 2, "e4m3")
    real = np.einsum('btn,kn->tbk', fq, unpack_weight(wcos_words, wcos_scales, FMT).T)
    imag = np.einsum('btn,kn->tbk', fq, unpack_weight(wsin_words, wsin_scales, FMT).T)
    return real, -imag

@@ -1,0 +1,141 @@
+from contextlib import ExitStack
+
+import concourse.mybir as mybir
+from concourse.masks import make_identity
+
+BF16 = mybir.dt.bfloat16
+F32 = mybir.dt.float32
+I32 = mybir.dt.int32
+U32 = mybir.dt.uint32
+U8 = mybir.dt.uint8
+FP8X4 = mybir.dt.float8_e4m3fn_x4
+
+P = 128
+PACK = 4
+K_PASS = P * PACK
+N_FFT = 1024
+PASSES = N_FFT // K_PASS
+SIGNALS = 16
+FRAMES = 128
+STRIDE = N_FFT + 1
+N_TILE = 512
+N_TILES = N_FFT // N_TILE
+PAIR = 2
+PAIRS = SIGNALS // PAIR
+QUADS = 4
+WORDS = N_FFT // 2
+
+FLOPS = 2 * SIGNALS * FRAMES * N_FFT * (2 * N_FFT)
+
+
+def tile_dftlayer_kernel(tc, x, wsin_words, wsin_scales, wcos_words, wcos_scales, out_0, out_1):
+    nc = tc.nc
+    transforms = (
+        (wcos_words, wcos_scales, out_0, 1.0),
+        (wsin_words, wsin_scales, out_1, -1.0),
+    )
+    frames = x[0].rearrange("b (t s) -> b t s", s=STRIDE)
+
+    with ExitStack() as ctx:
+        ctx.enter_context(tc.manual_schedule())
+        keep = ctx.enter_context(tc.tile_pool(name="keep", bufs=1))
+        work = ctx.enter_context(tc.tile_pool(name="work", bufs=2 * PAIR))
+        stage = ctx.enter_context(tc.tile_pool(name="stage", bufs=2 * PAIRS))
+        xt_banks = ctx.enter_context(tc.psum_pool(name="xt_banks", bufs=PAIR))
+        acc_banks = ctx.enter_context(tc.psum_pool(name="acc_banks", bufs=8 - PAIR))
+
+        x_tiles = [keep.tile([P, N_FFT], BF16, name="x%d" % b) for b in range(SIGNALS)]
+        w_words = [
+            [keep.tile([P, N_FFT], I32, name="w%d_words%d" % (w, g), align_bytes=64) for g in range(PASSES)]
+            for w in range(2)
+        ]
+        w_planes = [keep.tile([P, PASSES, N_FFT], U8, name="w%d_planes" % w, align_bytes=64) for w in range(2)]
+        ident = keep.tile([P, P], F32, name="ident")
+
+        for w in range(2):
+            nc.vector.memset(w_planes[w][:].bitcast(I32), 0)
+        make_identity(nc, ident[:])
+
+        def load_frames(b):
+            nc.sync.dma_start(out=x_tiles[b][:], in_=frames[b, :, 0:N_FFT])
+
+        def load_weight(w):
+            words, scales = transforms[w][0], transforms[w][1]
+            for quad in range(QUADS):
+                nc.sync.dma_start(
+                    out=w_planes[w][32 * quad : 32 * quad + 4, :, :].bitcast(I32),
+                    in_=scales[:, 4 * quad : 4 * quad + 4, :].rearrange("g r n -> r g n").bitcast(I32),
+                )
+            for g in range(PASSES):
+                nc.sync.dma_start(
+                    out=w_words[w][g][:],
+                    in_=words[g].rearrange("p n t -> p (n t)").bitcast(I32),
+                )
+
+        for b in range(PAIR):
+            load_frames(b)
+        load_weight(0)
+        for b in range(PAIR, 2 * PAIR):
+            load_frames(b)
+        load_weight(1)
+        for b in range(2 * PAIR, SIGNALS):
+            load_frames(b)
+
+        codes = {}
+        planes = {}
+
+        def prepare(pair):
+            grouped = {}
+            for b in range(PAIR * pair, PAIR * pair + PAIR):
+                x_words = x_tiles[b][:].bitcast(F32)
+                xt = xt_banks.tile([P, 2, PASSES * FRAMES], F32, name="xt")
+                for g in range(PASSES):
+                    for u in range(2):
+                        nc.tensor.transpose(
+                            xt[:, u, g * FRAMES : (g + 1) * FRAMES],
+                            x_words[:, (WORDS // PASSES) * g + u : (WORDS // PASSES) * (g + 1) : 2],
+                            ident[:],
+                        )
+                grouped[b] = work.tile([P, PASSES * FRAMES, PACK], BF16, name="grouped", align_bytes=64)
+                copy = nc.vector.tensor_copy if b % 2 == 0 else nc.scalar.copy
+                copy(out=grouped[b][:].bitcast(F32), in_=xt[:].rearrange("p u c -> p c u"))
+            for b in range(PAIR * pair, PAIR * pair + PAIR):
+                codes[b] = work.tile([P, PASSES * FRAMES], U32, name="codes", align_bytes=64)
+                planes[b] = work.tile([P, PASSES * FRAMES], U8, name="planes", align_bytes=64)
+                nc.vector.quantize_mx(
+                    out=codes[b][:].bitcast(FP8X4),
+                    scales=planes[b][:],
+                    in_=grouped[b][:].rearrange("p c j -> p (c j)"),
+                )
+
+        def multiply(pair, w):
+            out, sign = transforms[w][2], transforms[w][3]
+            result = stage.tile([P, PAIR, N_FFT], F32, name="result")
+            for i in range(PAIR):
+                b = PAIR * pair + i
+                for n in range(N_TILES):
+                    n_cols = slice(n * N_TILE, (n + 1) * N_TILE)
+                    acc = acc_banks.tile([P, N_TILE], F32, name="acc")
+                    for g in range(PASSES):
+                        t_cols = slice(g * FRAMES, (g + 1) * FRAMES)
+                        nc.tensor.matmul_mx(
+                            out=acc[:],
+                            lhsT=codes[b][:, t_cols].bitcast(FP8X4),
+                            lhsT_scale=planes[b][:, t_cols],
+                            rhs=w_words[w][g][:, n_cols].bitcast(FP8X4),
+                            rhs_scale=w_planes[w][:, g, n_cols],
+                            start=(g == 0),
+                            stop=(g == PASSES - 1),
+                        )
+                    if n % 2 == 0:
+                        nc.vector.tensor_scalar_mul(out=result[:, i, n_cols], in0=acc[:], scalar1=sign)
+                    else:
+                        nc.scalar.mul(out=result[:, i, n_cols], in_=acc[:], mul=sign)
+            nc.sync.dma_start(out=out[:, PAIR * pair : PAIR * pair + PAIR, :], in_=result[:])
+
+        prepare(0)
+        for pair in range(PAIRS):
+            multiply(pair, 0)
+            if pair + 1 < PAIRS:
+                prepare(pair + 1)
+            multiply(pair, 1)

@@ -81,21 +81,24 @@ def tile_dftlayer_kernel(tc, x, wsin_words, wsin_scales, wcos_words, wcos_scales
         for b in range(2 * PAIR, SIGNALS):
             load_frames(b)
 
+        sorted_words = {}
         codes = {}
         planes = {}
+
+        def sort_words(pair):
+            for b in range(PAIR * pair, PAIR * pair + PAIR):
+                sorted_words[b] = work.tile([P, 2, WORDS // 2], F32, name="sorted_words")
+                copy = nc.vector.tensor_copy if b % 2 == 0 else nc.scalar.copy
+                copy(out=sorted_words[b][:], in_=x_tiles[b][:].bitcast(F32).rearrange("p (c u) -> p u c", u=2))
 
         def prepare(pair):
             grouped = {}
             for b in range(PAIR * pair, PAIR * pair + PAIR):
-                x_words = x_tiles[b][:].bitcast(F32)
                 xt = xt_banks.tile([P, 2, PASSES * FRAMES], F32, name="xt")
                 for g in range(PASSES):
                     for u in range(2):
-                        nc.tensor.transpose(
-                            xt[:, u, g * FRAMES : (g + 1) * FRAMES],
-                            x_words[:, (WORDS // PASSES) * g + u : (WORDS // PASSES) * (g + 1) : 2],
-                            ident[:],
-                        )
+                        t_cols = slice(g * FRAMES, (g + 1) * FRAMES)
+                        nc.tensor.transpose(xt[:, u, t_cols], sorted_words[b][:, u, t_cols], ident[:])
                 grouped[b] = work.tile([P, PASSES * FRAMES, PACK], BF16, name="grouped", align_bytes=64)
                 copy = nc.vector.tensor_copy if b % 2 == 0 else nc.scalar.copy
                 copy(out=grouped[b][:].bitcast(F32), in_=xt[:].rearrange("p u c -> p c u"))
@@ -111,6 +114,7 @@ def tile_dftlayer_kernel(tc, x, wsin_words, wsin_scales, wcos_words, wcos_scales
         def multiply(pair, w):
             out, sign = transforms[w][2], transforms[w][3]
             result = stage.tile([P, PAIR, N_FFT], F32, name="result")
+            last = pair == PAIRS - 1
             for i in range(PAIR):
                 b = PAIR * pair + i
                 for n in range(N_TILES):
@@ -131,10 +135,16 @@ def tile_dftlayer_kernel(tc, x, wsin_words, wsin_scales, wcos_words, wcos_scales
                         nc.vector.tensor_scalar_mul(out=result[:, i, n_cols], in0=acc[:], scalar1=sign)
                     else:
                         nc.scalar.mul(out=result[:, i, n_cols], in_=acc[:], mul=sign)
-            nc.sync.dma_start(out=out[:, PAIR * pair : PAIR * pair + PAIR, :], in_=result[:])
+                if last:
+                    nc.sync.dma_start(out=out[:, b, :], in_=result[:, i, :])
+            if not last:
+                nc.sync.dma_start(out=out[:, PAIR * pair : PAIR * pair + PAIR, :], in_=result[:])
 
+        sort_words(0)
         prepare(0)
         for pair in range(PAIRS):
+            if pair + 1 < PAIRS:
+                sort_words(pair + 1)
             multiply(pair, 0)
             if pair + 1 < PAIRS:
                 prepare(pair + 1)

@@ -113,6 +113,7 @@ def tile_dftlayer_kernel(tc, x, wsin_words, wsin_scales, wcos_words, wcos_scales
 
         def multiply(pair, w):
             out, sign = transforms[w][2], transforms[w][3]
+            queue = nc.sync if w == 0 else nc.scalar
             result = stage.tile([P, PAIR, N_FFT], F32, name="result")
             last = pair == PAIRS - 1
             for i in range(PAIR):
@@ -136,9 +137,9 @@ def tile_dftlayer_kernel(tc, x, wsin_words, wsin_scales, wcos_words, wcos_scales
                     else:
                         nc.scalar.mul(out=result[:, i, n_cols], in_=acc[:], mul=sign)
                 if last:
-                    nc.sync.dma_start(out=out[:, b, :], in_=result[:, i, :])
+                    queue.dma_start(out=out[:, b, :], in_=result[:, i, :])
             if not last:
-                nc.sync.dma_start(out=out[:, PAIR * pair : PAIR * pair + PAIR, :], in_=result[:])
+                queue.dma_start(out=out[:, PAIR * pair : PAIR * pair + PAIR, :], in_=result[:])
 
         sort_words(0)
         prepare(0)

@@ -22,7 +22,6 @@ N_TILE = 512
 N_TILES = N_FFT // N_TILE
 PAIR = 2
 PAIRS = SIGNALS // PAIR
-QUADS = 4
 WORDS = N_FFT // 2
 
 FLOPS = 2 * SIGNALS * FRAMES * N_FFT * (2 * N_FFT)
@@ -61,10 +60,10 @@ def tile_dftlayer_kernel(tc, x, wsin_words, wsin_scales, wcos_words, wcos_scales
 
         def load_weight(w):
             words, scales = transforms[w][0], transforms[w][1]
-            for quad in range(QUADS):
+            for r in range(4):
                 nc.sync.dma_start(
-                    out=w_planes[w][32 * quad : 32 * quad + 4, :, :].bitcast(I32),
-                    in_=scales[:, 4 * quad : 4 * quad + 4, :].rearrange("g r n -> r g n").bitcast(I32),
+                    out=w_planes[w][r:P:32, :, :].bitcast(I32),
+                    in_=scales[:, r:16:4, :].rearrange("g q n -> q g n").bitcast(I32),
                 )
             for g in range(PASSES):
                 nc.sync.dma_start(

@@ -22,6 +22,8 @@ N_TILE = 512
 N_TILES = N_FFT // N_TILE
 PAIR = 2
 PAIRS = SIGNALS // PAIR
+RUN = 2
+SLOTS = FRAMES // RUN
 WORDS = N_FFT // 2
 
 FLOPS = 2 * SIGNALS * FRAMES * N_FFT * (2 * N_FFT)
@@ -33,7 +35,7 @@ def tile_dftlayer_kernel(tc, x, wsin_words, wsin_scales, wcos_words, wcos_scales
         (wcos_words, wcos_scales, out_0, 1.0),
         (wsin_words, wsin_scales, out_1, -1.0),
     )
-    frames = x[0].rearrange("b (t s) -> b t s", s=STRIDE)
+    runs = x[0].rearrange("b (h s) -> (b h) s", s=RUN * STRIDE)
 
     with ExitStack() as ctx:
         ctx.enter_context(tc.manual_schedule())
@@ -43,7 +45,7 @@ def tile_dftlayer_kernel(tc, x, wsin_words, wsin_scales, wcos_words, wcos_scales
         xt_banks = ctx.enter_context(tc.psum_pool(name="xt_banks", bufs=PAIR))
         acc_banks = ctx.enter_context(tc.psum_pool(name="acc_banks", bufs=8 - PAIR))
 
-        x_tiles = [keep.tile([P, N_FFT], BF16, name="x%d" % b) for b in range(SIGNALS)]
+        x_tiles = [keep.tile([P, RUN * STRIDE], BF16, name="x%d" % pair) for pair in range(PAIRS)]
         w_words = [
             [keep.tile([P, N_FFT], I32, name="w%d_words%d" % (w, g), align_bytes=64) for g in range(PASSES)]
             for w in range(2)
@@ -55,8 +57,8 @@ def tile_dftlayer_kernel(tc, x, wsin_words, wsin_scales, wcos_words, wcos_scales
             nc.vector.memset(w_planes[w][:].bitcast(I32), 0)
         make_identity(nc, ident[:])
 
-        def load_frames(b):
-            nc.sync.dma_start(out=x_tiles[b][:], in_=frames[b, :, 0:N_FFT])
+        def load_frames(pair):
+            nc.sync.dma_start(out=x_tiles[pair][:], in_=runs[pair * P : (pair + 1) * P, :])
 
         def load_weight(w):
             words, scales = transforms[w][0], transforms[w][1]
@@ -71,43 +73,49 @@ def tile_dftlayer_kernel(tc, x, wsin_words, wsin_scales, wcos_words, wcos_scales
                     in_=words[g].rearrange("p n t -> p (n t)").bitcast(I32),
                 )
 
-        for b in range(PAIR):
-            load_frames(b)
+        load_frames(0)
         load_weight(0)
-        for b in range(PAIR, 2 * PAIR):
-            load_frames(b)
+        load_frames(1)
         load_weight(1)
-        for b in range(2 * PAIR, SIGNALS):
-            load_frames(b)
+        for pair in range(2, PAIRS):
+            load_frames(pair)
 
         sorted_words = {}
         codes = {}
         planes = {}
 
         def sort_words(pair):
-            for b in range(PAIR * pair, PAIR * pair + PAIR):
-                sorted_words[b] = work.tile([P, 2, WORDS // 2], F32, name="sorted_words")
-                copy = nc.vector.tensor_copy if b % 2 == 0 else nc.scalar.copy
-                copy(out=sorted_words[b][:], in_=x_tiles[b][:].bitcast(F32).rearrange("p (c u) -> p u c", u=2))
+            sorted_words[pair] = work.tile([P, RUN, 2, WORDS // 2], F32, name="sorted_words")
+            nc.vector.tensor_copy(
+                out=sorted_words[pair][:, 0, :, :],
+                in_=x_tiles[pair][:, 0:N_FFT].bitcast(F32).rearrange("p (c u) -> p u c", u=2),
+            )
+            nc.scalar.copy(
+                out=sorted_words[pair][:, 1, :, :].rearrange("p u c -> p (u c)").bitcast(BF16)
+                .rearrange("p (u c e) -> p u c e", u=2, e=2),
+                in_=x_tiles[pair][:, STRIDE : STRIDE + N_FFT].rearrange("p (c u e) -> p u c e", u=2, e=2),
+            )
 
         def prepare(pair):
             grouped = {}
-            for b in range(PAIR * pair, PAIR * pair + PAIR):
-                xt = xt_banks.tile([P, 2, PASSES * FRAMES], F32, name="xt")
-                for g in range(PASSES):
+            for g in range(PASSES):
+                xt = xt_banks.tile([P, RUN * 2, P], F32, name="xt")
+                for r in range(RUN):
                     for u in range(2):
-                        t_cols = slice(g * FRAMES, (g + 1) * FRAMES)
-                        nc.tensor.transpose(xt[:, u, t_cols], sorted_words[b][:, u, t_cols], ident[:])
-                grouped[b] = work.tile([P, PASSES * FRAMES, PACK], BF16, name="grouped", align_bytes=64)
-                copy = nc.vector.tensor_copy if b % 2 == 0 else nc.scalar.copy
-                copy(out=grouped[b][:].bitcast(F32), in_=xt[:].rearrange("p u c -> p c u"))
-            for b in range(PAIR * pair, PAIR * pair + PAIR):
-                codes[b] = work.tile([P, PASSES * FRAMES], U32, name="codes", align_bytes=64)
-                planes[b] = work.tile([P, PASSES * FRAMES], U8, name="planes", align_bytes=64)
+                        nc.tensor.transpose(xt[:, 2 * r + u, :], sorted_words[pair][:, r, u, g * P : (g + 1) * P], ident[:])
+                grouped[g] = work.tile([P, P, RUN * PACK], BF16, name="grouped", align_bytes=64)
+                copy = nc.vector.tensor_copy if g % 2 == 0 else nc.scalar.copy
+                copy(
+                    out=grouped[g][:].rearrange("p c j -> p (c j)").bitcast(F32).rearrange("p (c j) -> p c j", j=RUN * 2),
+                    in_=xt[:].rearrange("p j c -> p c j"),
+                )
+            for g in range(PASSES):
+                codes[pair, g] = work.tile([P, PAIR * FRAMES], U32, name="codes", align_bytes=64)
+                planes[pair, g] = work.tile([P, PAIR * FRAMES], U8, name="planes", align_bytes=64)
                 nc.vector.quantize_mx(
-                    out=codes[b][:].bitcast(FP8X4),
-                    scales=planes[b][:],
-                    in_=grouped[b][:].rearrange("p c j -> p (c j)"),
+                    out=codes[pair, g][:].bitcast(FP8X4),
+                    scales=planes[pair, g][:],
+                    in_=grouped[g][:].rearrange("p c j -> p (c j)"),
                 )
 
         def multiply(pair, w):
@@ -121,11 +129,11 @@ def tile_dftlayer_kernel(tc, x, wsin_words, wsin_scales, wcos_words, wcos_scales
                     n_cols = slice(n * N_TILE, (n + 1) * N_TILE)
                     acc = acc_banks.tile([P, N_TILE], F32, name="acc")
                     for g in range(PASSES):
-                        t_cols = slice(g * FRAMES, (g + 1) * FRAMES)
+                        t_cols = slice(i * FRAMES, (i + 1) * FRAMES)
                         nc.tensor.matmul_mx(
                             out=acc[:],
-                            lhsT=codes[b][:, t_cols].bitcast(FP8X4),
-                            lhsT_scale=planes[b][:, t_cols],
+                            lhsT=codes[pair, g][:, t_cols].bitcast(FP8X4),
+                            lhsT_scale=planes[pair, g][:, t_cols],
                             rhs=w_words[w][g][:, n_cols].bitcast(FP8X4),
                             rhs_scale=w_planes[w][:, g, n_cols],
                             start=(g == 0),

@@ -23,8 +23,8 @@ N_TILES = N_FFT // N_TILE
 PAIR = 2
 PAIRS = SIGNALS // PAIR
 RUN = 2
-SLOTS = FRAMES // RUN
 WORDS = N_FFT // 2
+PASS_WORDS = K_PASS // 2
 
 FLOPS = 2 * SIGNALS * FRAMES * N_FFT * (2 * N_FFT)
 
@@ -35,17 +35,19 @@ def tile_dftlayer_kernel(tc, x, wsin_words, wsin_scales, wcos_words, wcos_scales
         (wcos_words, wcos_scales, out_0, 1.0),
         (wsin_words, wsin_scales, out_1, -1.0),
     )
+    frames = x[0].rearrange("b (t s) -> b t s", s=STRIDE)
     runs = x[0].rearrange("b (h s) -> (b h) s", s=RUN * STRIDE)
 
     with ExitStack() as ctx:
         ctx.enter_context(tc.manual_schedule())
         keep = ctx.enter_context(tc.tile_pool(name="keep", bufs=1))
-        work = ctx.enter_context(tc.tile_pool(name="work", bufs=2 * PAIR))
+        work = ctx.enter_context(tc.tile_pool(name="work", bufs=2))
         stage = ctx.enter_context(tc.tile_pool(name="stage", bufs=2 * PAIRS))
-        xt_banks = ctx.enter_context(tc.psum_pool(name="xt_banks", bufs=PAIR))
-        acc_banks = ctx.enter_context(tc.psum_pool(name="acc_banks", bufs=8 - PAIR))
+        xt_banks = ctx.enter_context(tc.psum_pool(name="xt_banks", bufs=PASSES))
+        acc_banks = ctx.enter_context(tc.psum_pool(name="acc_banks", bufs=8 - PASSES))
 
-        x_tiles = [keep.tile([P, RUN * STRIDE], BF16, name="x%d" % pair) for pair in range(PAIRS)]
+        head_tiles = [keep.tile([P, N_FFT], BF16, name="head%d" % b) for b in range(PAIR)]
+        x_tiles = [keep.tile([P, RUN * STRIDE], BF16, name="x%d" % pair) for pair in range(1, PAIRS)]
         w_words = [
             [keep.tile([P, N_FFT], I32, name="w%d_words%d" % (w, g), align_bytes=64) for g in range(PASSES)]
             for w in range(2)
@@ -56,9 +58,6 @@ def tile_dftlayer_kernel(tc, x, wsin_words, wsin_scales, wcos_words, wcos_scales
         for w in range(2):
             nc.vector.memset(w_planes[w][:].bitcast(I32), 0)
         make_identity(nc, ident[:])
-
-        def load_frames(pair):
-            nc.sync.dma_start(out=x_tiles[pair][:], in_=runs[pair * P : (pair + 1) * P, :])
 
         def load_weight(w):
             words, scales = transforms[w][0], transforms[w][1]
@@ -73,87 +72,163 @@ def tile_dftlayer_kernel(tc, x, wsin_words, wsin_scales, wcos_words, wcos_scales
                     in_=words[g].rearrange("p n t -> p (n t)").bitcast(I32),
                 )
 
-        load_frames(0)
+        def load_runs(pair):
+            nc.sync.dma_start(out=x_tiles[pair - 1][:], in_=runs[pair * P : (pair + 1) * P, :])
+
+        for b in range(PAIR):
+            nc.sync.dma_start(out=head_tiles[b][:], in_=frames[b, :, 0:N_FFT])
         load_weight(0)
-        load_frames(1)
+        load_runs(1)
         load_weight(1)
         for pair in range(2, PAIRS):
-            load_frames(pair)
+            load_runs(pair)
 
         sorted_words = {}
+        xts = {}
+        grouped = {}
         codes = {}
         planes = {}
 
-        def sort_words(pair):
-            sorted_words[pair] = work.tile([P, RUN, 2, WORDS // 2], F32, name="sorted_words")
-            nc.vector.tensor_copy(
-                out=sorted_words[pair][:, 0, :, :],
-                in_=x_tiles[pair][:, 0:N_FFT].bitcast(F32).rearrange("p (c u) -> p u c", u=2),
-            )
-            nc.scalar.copy(
-                out=sorted_words[pair][:, 1, :, :].rearrange("p u c -> p (u c)").bitcast(BF16)
-                .rearrange("p (u c e) -> p u c e", u=2, e=2),
-                in_=x_tiles[pair][:, STRIDE : STRIDE + N_FFT].rearrange("p (c u e) -> p u c e", u=2, e=2),
-            )
 
-        def prepare(pair):
-            grouped = {}
+        def new_codes(pair, g):
+            codes[pair, g] = work.tile([P, PAIR * FRAMES], U32, name="codes%d" % g, align_bytes=64)
+            planes[pair, g] = work.tile([P, PAIR * FRAMES], U8, name="planes%d" % g, align_bytes=64)
+
+        def prepare_head():
+            copies = (nc.vector.tensor_copy, nc.scalar.copy)
+            pieces = [(b, g) for b in range(PAIR) for g in range(PASSES)]
             for g in range(PASSES):
-                xt = xt_banks.tile([P, RUN * 2, P], F32, name="xt")
+                new_codes(0, g)
+            for b, g in pieces:
+                sorted_words[b, g] = keep.tile([P, 2, P], F32, name="head_words%d%d" % (b, g))
+                copies[g](
+                    out=sorted_words[b, g][:],
+                    in_=head_tiles[b][:, g * K_PASS : (g + 1) * K_PASS].bitcast(F32).rearrange("p (c u) -> p u c", u=2),
+                )
+            for b, g in pieces:
+                xts[b, g] = acc_banks.tile([P, 2, P], F32, name="acc")
+                for u in range(2):
+                    nc.tensor.transpose(xts[b, g][:, u, :], sorted_words[b, g][:, u, :], ident[:])
+            for b, g in pieces:
+                grouped[b, g] = keep.tile([P, P, PACK], BF16, name="head_grouped%d%d" % (b, g), align_bytes=64)
+                copies[g](
+                    out=grouped[b, g][:].rearrange("p c j -> p (c j)").bitcast(F32).rearrange("p (c u) -> p c u", u=2),
+                    in_=xts[b, g][:].rearrange("p u c -> p c u"),
+                )
+            for b, g in pieces:
+                t_cols = slice(b * FRAMES, (b + 1) * FRAMES)
+                nc.vector.quantize_mx(
+                    out=codes[0, g][:, t_cols].bitcast(FP8X4),
+                    scales=planes[0, g][:, t_cols],
+                    in_=grouped[b, g][:].rearrange("p c j -> p (c j)"),
+                )
+
+        def sort_words(pair):
+            for r in range(RUN):
+                sorted_words[pair, r] = work.tile([P, 2, WORDS // 2], F32, name="sorted_words%d" % r)
+                samples = x_tiles[pair - 1][:, r * STRIDE : r * STRIDE + N_FFT]
+                if r == 0:
+                    nc.scalar.copy(
+                        out=sorted_words[pair, r][:], in_=samples.bitcast(F32).rearrange("p (c u) -> p u c", u=2)
+                    )
+                else:
+                    nc.vector.tensor_copy(
+                        out=sorted_words[pair, r][:].rearrange("p u c -> p (u c)").bitcast(BF16)
+                        .rearrange("p (u c e) -> p u c e", u=2, e=2),
+                        in_=samples.rearrange("p (c u e) -> p u c e", u=2, e=2),
+                    )
+
+        def transpose_words(pair):
+            for g in range(PASSES):
+                xts[pair, g] = xt_banks.tile([P, RUN * 2, P], F32, name="xt")
                 for r in range(RUN):
                     for u in range(2):
-                        nc.tensor.transpose(xt[:, 2 * r + u, :], sorted_words[pair][:, r, u, g * P : (g + 1) * P], ident[:])
-                grouped[g] = work.tile([P, P, RUN * PACK], BF16, name="grouped", align_bytes=64)
-                copy = nc.vector.tensor_copy if g % 2 == 0 else nc.scalar.copy
-                copy(
-                    out=grouped[g][:].rearrange("p c j -> p (c j)").bitcast(F32).rearrange("p (c j) -> p c j", j=RUN * 2),
-                    in_=xt[:].rearrange("p j c -> p c j"),
-                )
+                        nc.tensor.transpose(
+                            xts[pair, g][:, 2 * r + u, :], sorted_words[pair, r][:, u, g * P : (g + 1) * P], ident[:]
+                        )
+
+        def group_words(pair):
             for g in range(PASSES):
-                codes[pair, g] = work.tile([P, PAIR * FRAMES], U32, name="codes", align_bytes=64)
-                planes[pair, g] = work.tile([P, PAIR * FRAMES], U8, name="planes", align_bytes=64)
+                grouped[pair, g] = work.tile([P, P, RUN * PACK], BF16, name="grouped%d" % g, align_bytes=64)
+                copy = nc.vector.tensor_copy if g == 0 else nc.scalar.copy
+                copy(
+                    out=grouped[pair, g][:].rearrange("p c j -> p (c j)").bitcast(F32)
+                    .rearrange("p (c j) -> p c j", j=RUN * 2),
+                    in_=xts[pair, g][:].rearrange("p j c -> p c j"),
+                )
+
+        def quantise(pair):
+            for g in range(PASSES):
+                new_codes(pair, g)
                 nc.vector.quantize_mx(
                     out=codes[pair, g][:].bitcast(FP8X4),
                     scales=planes[pair, g][:],
-                    in_=grouped[g][:].rearrange("p c j -> p (c j)"),
+                    in_=grouped[pair, g][:].rearrange("p c j -> p (c j)"),
                 )
 
-        def multiply(pair, w):
+        results = {}
+
+        def one_pass(pair, w, i, n, g, acc):
+            t_cols = slice(i * FRAMES, (i + 1) * FRAMES)
+            n_cols = slice(n * N_TILE, (n + 1) * N_TILE)
+            nc.tensor.matmul_mx(
+                out=acc[:],
+                lhsT=codes[pair, g][:, t_cols].bitcast(FP8X4),
+                lhsT_scale=planes[pair, g][:, t_cols],
+                rhs=w_words[w][g][:, n_cols].bitcast(FP8X4),
+                rhs_scale=w_planes[w][:, g, n_cols],
+                start=(g == 0),
+                stop=(g == PASSES - 1),
+            )
+
+        def empty(pair, w, i, accs):
             out, sign = transforms[w][2], transforms[w][3]
             queue = nc.sync if w == 0 else nc.scalar
-            result = stage.tile([P, PAIR, N_FFT], F32, name="result")
-            last = pair == PAIRS - 1
-            for i in range(PAIR):
-                b = PAIR * pair + i
-                for n in range(N_TILES):
-                    n_cols = slice(n * N_TILE, (n + 1) * N_TILE)
-                    acc = acc_banks.tile([P, N_TILE], F32, name="acc")
-                    for g in range(PASSES):
-                        t_cols = slice(i * FRAMES, (i + 1) * FRAMES)
-                        nc.tensor.matmul_mx(
-                            out=acc[:],
-                            lhsT=codes[pair, g][:, t_cols].bitcast(FP8X4),
-                            lhsT_scale=planes[pair, g][:, t_cols],
-                            rhs=w_words[w][g][:, n_cols].bitcast(FP8X4),
-                            rhs_scale=w_planes[w][:, g, n_cols],
-                            start=(g == 0),
-                            stop=(g == PASSES - 1),
-                        )
-                    if n % 2 == 0:
-                        nc.vector.tensor_scalar_mul(out=result[:, i, n_cols], in0=acc[:], scalar1=sign)
-                    else:
-                        nc.scalar.mul(out=result[:, i, n_cols], in_=acc[:], mul=sign)
-                if last:
-                    queue.dma_start(out=out[:, b, :], in_=result[:, i, :])
-            if not last:
-                queue.dma_start(out=out[:, PAIR * pair : PAIR * pair + PAIR, :], in_=result[:])
+            if i == 0:
+                results[w] = stage.tile([P, PAIR, N_FFT], F32, name="result")
+            result = results[w]
+            b = PAIR * pair + i
+            for n in range(N_TILES):
+                n_cols = slice(n * N_TILE, (n + 1) * N_TILE)
+                if n % 2 == 0:
+                    nc.vector.tensor_scalar_mul(out=result[:, i, n_cols], in0=accs[n][:], scalar1=sign)
+                else:
+                    nc.scalar.mul(out=result[:, i, n_cols], in_=accs[n][:], mul=sign)
+            if pair == PAIRS - 1:
+                queue.dma_start(out=out[:, b, :], in_=result[:, i, :])
+            elif i == PAIR - 1:
+                queue.dma_start(out=out[:, b - 1 : b + 1, :], in_=result[:])
 
-        sort_words(0)
-        prepare(0)
+        def new_accs():
+            return [acc_banks.tile([P, N_TILE], F32, name="acc") for n in range(N_TILES)]
+
+        def multiply(pair, w, i):
+            accs = new_accs()
+            for n in range(N_TILES):
+                for g in range(PASSES):
+                    one_pass(pair, w, i, n, g, accs[n])
+            return accs
+
+        prepare_head()
         for pair in range(PAIRS):
-            if pair + 1 < PAIRS:
+            more = pair + 1 < PAIRS
+            if more:
                 sort_words(pair + 1)
-            multiply(pair, 0)
-            if pair + 1 < PAIRS:
-                prepare(pair + 1)
-            multiply(pair, 1)
+            if pair == 0:
+                accs = [new_accs() for i in range(PAIR)]
+                for g in range(PASSES):
+                    for i in range(PAIR):
+                        for n in range(N_TILES):
+                            one_pass(pair, 0, i, n, g, accs[i][n])
+                for i in range(PAIR):
+                    empty(pair, 0, i, accs[i])
+            else:
+                for i in range(PAIR):
+                    empty(pair, 0, i, multiply(pair, 0, i))
+            if more:
+                transpose_words(pair + 1)
+                group_words(pair + 1)
+            empty(pair, 1, 0, multiply(pair, 1, 0))
+            if more:
+                quantise(pair + 1)
+            empty(pair, 1, 1, multiply(pair, 1, 1))

@@ -22,6 +22,7 @@ N_TILE = 512
 N_TILES = N_FFT // N_TILE
 PAIR = 2
 PAIRS = SIGNALS // PAIR
+SINGLE_PAIRS = 3
 RUN = 2
 WORDS = N_FFT // 2
 PASS_WORDS = K_PASS // 2
@@ -194,7 +195,7 @@ def tile_dftlayer_kernel(tc, x, wsin_words, wsin_scales, wcos_words, wcos_scales
                     nc.vector.tensor_scalar_mul(out=result[:, i, n_cols], in0=accs[n][:], scalar1=sign)
                 else:
                     nc.scalar.mul(out=result[:, i, n_cols], in_=accs[n][:], mul=sign)
-            if pair == PAIRS - 1:
+            if pair >= PAIRS - SINGLE_PAIRS:
                 queue.dma_start(out=out[:, b, :], in_=result[:, i, :])
             elif i == PAIR - 1:
                 queue.dma_start(out=out[:, b - 1 : b + 1, :], in_=result[:])

from contextlib import ExitStack

import concourse.mybir as mybir
from concourse.masks import make_identity

BF16 = mybir.dt.bfloat16
F32 = mybir.dt.float32
I32 = mybir.dt.int32
U32 = mybir.dt.uint32
U8 = mybir.dt.uint8
FP8X4 = mybir.dt.float8_e4m3fn_x4

P = 128
PACK = 4
K_PASS = P * PACK
N_FFT = 1024
PASSES = N_FFT // K_PASS
SIGNALS = 16
FRAMES = 128
STRIDE = N_FFT + 1
N_TILE = 512
N_TILES = N_FFT // N_TILE
PAIR = 2
PAIRS = SIGNALS // PAIR
SINGLE_PAIRS = 3
RUN = 2
WORDS = N_FFT // 2
PASS_WORDS = K_PASS // 2

FLOPS = 2 * SIGNALS * FRAMES * N_FFT * (2 * N_FFT)


def tile_dftlayer_kernel(tc, x, wsin_words, wsin_scales, wcos_words, wcos_scales, out_0, out_1):
    nc = tc.nc
    transforms = (
        (wcos_words, wcos_scales, out_0, 1.0),
        (wsin_words, wsin_scales, out_1, -1.0),
    )
    frames = x[0].rearrange("b (t s) -> b t s", s=STRIDE)
    runs = x[0].rearrange("b (h s) -> (b h) s", s=RUN * STRIDE)

    with ExitStack() as ctx:
        ctx.enter_context(tc.manual_schedule())
        keep = ctx.enter_context(tc.tile_pool(name="keep", bufs=1))
        work = ctx.enter_context(tc.tile_pool(name="work", bufs=2))
        stage = ctx.enter_context(tc.tile_pool(name="stage", bufs=2 * PAIRS))
        xt_banks = ctx.enter_context(tc.psum_pool(name="xt_banks", bufs=PASSES))
        acc_banks = ctx.enter_context(tc.psum_pool(name="acc_banks", bufs=8 - PASSES))

        head_tiles = [keep.tile([P, N_FFT], BF16, name="head%d" % b) for b in range(PAIR)]
        x_tiles = [keep.tile([P, RUN * STRIDE], BF16, name="x%d" % pair) for pair in range(1, PAIRS)]
        w_words = [
            [keep.tile([P, N_FFT], I32, name="w%d_words%d" % (w, g), align_bytes=64) for g in range(PASSES)]
            for w in range(2)
        ]
        w_planes = [keep.tile([P, PASSES, N_FFT], U8, name="w%d_planes" % w, align_bytes=64) for w in range(2)]
        ident = keep.tile([P, P], F32, name="ident")

        for w in range(2):
            nc.vector.memset(w_planes[w][:].bitcast(I32), 0)
        make_identity(nc, ident[:])

        def load_weight(w):
            words, scales = transforms[w][0], transforms[w][1]
            for r in range(4):
                nc.sync.dma_start(
                    out=w_planes[w][r:P:32, :, :].bitcast(I32),
                    in_=scales[:, r:16:4, :].rearrange("g q n -> q g n").bitcast(I32),
                )
            for g in range(PASSES):
                nc.sync.dma_start(
                    out=w_words[w][g][:],
                    in_=words[g].rearrange("p n t -> p (n t)").bitcast(I32),
                )

        def load_runs(pair):
            nc.sync.dma_start(out=x_tiles[pair - 1][:], in_=runs[pair * P : (pair + 1) * P, :])

        for b in range(PAIR):
            nc.sync.dma_start(out=head_tiles[b][:], in_=frames[b, :, 0:N_FFT])
        load_weight(0)
        load_runs(1)
        load_weight(1)
        for pair in range(2, PAIRS):
            load_runs(pair)

        sorted_words = {}
        xts = {}
        grouped = {}
        codes = {}
        planes = {}


        def new_codes(pair, g):
            codes[pair, g] = work.tile([P, PAIR * FRAMES], U32, name="codes%d" % g, align_bytes=64)
            planes[pair, g] = work.tile([P, PAIR * FRAMES], U8, name="planes%d" % g, align_bytes=64)

        def prepare_head():
            copies = (nc.vector.tensor_copy, nc.scalar.copy)
            pieces = [(b, g) for b in range(PAIR) for g in range(PASSES)]
            for g in range(PASSES):
                new_codes(0, g)
            for b, g in pieces:
                sorted_words[b, g] = keep.tile([P, 2, P], F32, name="head_words%d%d" % (b, g))
                copies[g](
                    out=sorted_words[b, g][:],
                    in_=head_tiles[b][:, g * K_PASS : (g + 1) * K_PASS].bitcast(F32).rearrange("p (c u) -> p u c", u=2),
                )
            for b, g in pieces:
                xts[b, g] = acc_banks.tile([P, 2, P], F32, name="acc")
                for u in range(2):
                    nc.tensor.transpose(xts[b, g][:, u, :], sorted_words[b, g][:, u, :], ident[:])
            for b, g in pieces:
                grouped[b, g] = keep.tile([P, P, PACK], BF16, name="head_grouped%d%d" % (b, g), align_bytes=64)
                copies[g](
                    out=grouped[b, g][:].rearrange("p c j -> p (c j)").bitcast(F32).rearrange("p (c u) -> p c u", u=2),
                    in_=xts[b, g][:].rearrange("p u c -> p c u"),
                )
            for b, g in pieces:
                t_cols = slice(b * FRAMES, (b + 1) * FRAMES)
                nc.vector.quantize_mx(
                    out=codes[0, g][:, t_cols].bitcast(FP8X4),
                    scales=planes[0, g][:, t_cols],
                    in_=grouped[b, g][:].rearrange("p c j -> p (c j)"),
                )

        def sort_words(pair):
            for r in range(RUN):
                sorted_words[pair, r] = work.tile([P, 2, WORDS // 2], F32, name="sorted_words%d" % r)
                samples = x_tiles[pair - 1][:, r * STRIDE : r * STRIDE + N_FFT]
                if r == 0:
                    nc.scalar.copy(
                        out=sorted_words[pair, r][:], in_=samples.bitcast(F32).rearrange("p (c u) -> p u c", u=2)
                    )
                else:
                    nc.vector.tensor_copy(
                        out=sorted_words[pair, r][:].rearrange("p u c -> p (u c)").bitcast(BF16)
                        .rearrange("p (u c e) -> p u c e", u=2, e=2),
                        in_=samples.rearrange("p (c u e) -> p u c e", u=2, e=2),
                    )

        def transpose_words(pair):
            for g in range(PASSES):
                xts[pair, g] = xt_banks.tile([P, RUN * 2, P], F32, name="xt")
                for r in range(RUN):
                    for u in range(2):
                        nc.tensor.transpose(
                            xts[pair, g][:, 2 * r + u, :], sorted_words[pair, r][:, u, g * P : (g + 1) * P], ident[:]
                        )

        def group_words(pair):
            for g in range(PASSES):
                grouped[pair, g] = work.tile([P, P, RUN * PACK], BF16, name="grouped%d" % g, align_bytes=64)
                copy = nc.vector.tensor_copy if g == 0 else nc.scalar.copy
                copy(
                    out=grouped[pair, g][:].rearrange("p c j -> p (c j)").bitcast(F32)
                    .rearrange("p (c j) -> p c j", j=RUN * 2),
                    in_=xts[pair, g][:].rearrange("p j c -> p c j"),
                )

        def quantise(pair):
            for g in range(PASSES):
                new_codes(pair, g)
                nc.vector.quantize_mx(
                    out=codes[pair, g][:].bitcast(FP8X4),
                    scales=planes[pair, g][:],
                    in_=grouped[pair, g][:].rearrange("p c j -> p (c j)"),
                )

        results = {}

        def one_pass(pair, w, i, n, g, acc):
            t_cols = slice(i * FRAMES, (i + 1) * FRAMES)
            n_cols = slice(n * N_TILE, (n + 1) * N_TILE)
            nc.tensor.matmul_mx(
                out=acc[:],
                lhsT=codes[pair, g][:, t_cols].bitcast(FP8X4),
                lhsT_scale=planes[pair, g][:, t_cols],
                rhs=w_words[w][g][:, n_cols].bitcast(FP8X4),
                rhs_scale=w_planes[w][:, g, n_cols],
                start=(g == 0),
                stop=(g == PASSES - 1),
            )

        def empty(pair, w, i, accs):
            out, sign = transforms[w][2], transforms[w][3]
            queue = nc.sync if w == 0 else nc.scalar
            if i == 0:
                results[w] = stage.tile([P, PAIR, N_FFT], F32, name="result")
            result = results[w]
            b = PAIR * pair + i
            for n in range(N_TILES):
                n_cols = slice(n * N_TILE, (n + 1) * N_TILE)
                if n % 2 == 0:
                    nc.vector.tensor_scalar_mul(out=result[:, i, n_cols], in0=accs[n][:], scalar1=sign)
                else:
                    nc.scalar.mul(out=result[:, i, n_cols], in_=accs[n][:], mul=sign)
            if pair >= PAIRS - SINGLE_PAIRS:
                queue.dma_start(out=out[:, b, :], in_=result[:, i, :])
            elif i == PAIR - 1:
                queue.dma_start(out=out[:, b - 1 : b + 1, :], in_=result[:])

        def new_accs():
            return [acc_banks.tile([P, N_TILE], F32, name="acc") for n in range(N_TILES)]

        def multiply(pair, w, i):
            accs = new_accs()
            for n in range(N_TILES):
                for g in range(PASSES):
                    one_pass(pair, w, i, n, g, accs[n])
            return accs

        prepare_head()
        for pair in range(PAIRS):
            more = pair + 1 < PAIRS
            if more:
                sort_words(pair + 1)
            if pair == 0:
                accs = [new_accs() for i in range(PAIR)]
                for g in range(PASSES):
                    for i in range(PAIR):
                        for n in range(N_TILES):
                            one_pass(pair, 0, i, n, g, accs[i][n])
                for i in range(PAIR):
                    empty(pair, 0, i, accs[i])
            else:
                for i in range(PAIR):
                    empty(pair, 0, i, multiply(pair, 0, i))
            if more:
                transpose_words(pair + 1)
                group_words(pair + 1)
            empty(pair, 1, 0, multiply(pair, 1, 0))
            if more:
                quantise(pair + 1)
            empty(pair, 1, 1, multiply(pair, 1, 1))
